import numpy as np
import ml_dtypes


def mxq(x, axis, fmt="e4m3"):
    dtype, down = {"e4m3": (ml_dtypes.float8_e4m3fn, 7), "e5m2": (ml_dtypes.float8_e5m2, 14)}[fmt]
    v = np.moveaxis(np.asarray(x, np.float32).astype(ml_dtypes.bfloat16).astype(np.float64), axis, -1)
    blocks = v.reshape(v.shape[:-1] + (-1, 32))
    amax = np.abs(blocks).max(-1, keepdims=True)
    byte = np.maximum(np.where(amax > 0, np.frexp(amax)[1] - 1 + 127, 0) - down, 1)
    scale = np.exp2(byte - 127.0)
    codes = (blocks / scale).astype(np.float32).astype(dtype).astype(np.float64)
    return np.moveaxis((codes * scale).reshape(v.shape), -1, axis)


WIDE = False


def mx_kscale(k):
    if not WIDE:
        return np.ones(k)
    levels = np.array([10, -10, 5, -5, 0])
    a = np.random.permutation(np.resize(levels, k // 512 * 4)).reshape(k // 512, 4)
    idx = np.arange(k)
    return np.exp2(a[idx // 512, idx % 128 // 32])


BF16 = ml_dtypes.bfloat16


def bf(x):
    return np.asarray(x, np.float32).astype(BF16)


def f64(x):
    return np.asarray(x).astype(np.float64)


B, C, D, T, H, W, P = 1, 1024, 512, 8, 16, 16, 2
N = T * H * W
NP = T * (H // P) * (W // P)


def setup_inputs():
    s, t = mx_kscale(D), mx_kscale(NP)
    return {"theta_x": bf(np.random.standard_normal((B, D, N)) * 2.0 * s[None, :, None]),
            "phi_x": bf((1.03 + 0.7 * np.random.standard_normal((B, D, NP))) / s[None, :, None] * t[None, None, :]),
            "g_x": bf(0.15 * (1.03 + 0.7 * np.random.standard_normal((B, D, NP))) / t[None, None, :])}


def reference(theta_x, phi_x, g_x):
    f = (mxq(f64(theta_x), 1, "e4m3").transpose(0, 2, 1) @ mxq(f64(phi_x), 1, "e4m3")) / NP
    return mxq(f64(g_x), 2, "e4m3") @ mxq(f, 2, "e4m3").transpose(0, 2, 1)

@@ -1,0 +1,195 @@
+from contextlib import ExitStack
+
+import concourse.mybir as mybir
+from concourse.masks import make_identity
+
+BF16 = mybir.dt.bfloat16
+F32 = mybir.dt.float32
+U32 = mybir.dt.uint32
+U8 = mybir.dt.uint8
+FP8X4 = mybir.dt.float8_e4m3fn_x4
+COPY = mybir.ActivationFunctionType.Copy
+
+P = 128
+PACK = 4
+FEATURES = 512
+POSITIONS = 2048
+POOLED = 512
+CHUNK = 512
+N_CHUNKS = POSITIONS // CHUNK
+SUB = CHUNK // PACK
+N_BLOCKS = FEATURES // P
+SHARED_CHUNKS = 2
+
+FLOPS = 2 * POSITIONS * POOLED * FEATURES * 2
+
+
+def tile_nonlocalblocknd_pb_kernel(tc, theta_x, phi_x, g_x, out):
+    nc = tc.nc
+    theta_rows = theta_x[0].rearrange("(p j) n -> p j n", j=PACK)
+    phi_rows = phi_x[0].rearrange("(p j) m -> p j m", j=PACK)
+    g_rows = g_x[0].rearrange("(b p) m -> p b m", p=P)
+    out_rows = out[0].rearrange("(b p) n -> b p n", p=P)
+
+    with ExitStack() as ctx:
+        keep = ctx.enter_context(tc.tile_pool(name="keep", bufs=1))
+        f_banks = ctx.enter_context(tc.psum_pool(name="f_banks", bufs=4))
+        y_banks = ctx.enter_context(tc.psum_pool(name="y_banks", bufs=4))
+
+        phi_raw = keep.tile([P, PACK, POOLED], BF16)
+        g_raw = keep.tile([P, N_BLOCKS, POOLED], BF16)
+        theta_raw = [
+            keep.tile([P, PACK, CHUNK], BF16, name="theta_raw%d" % c) for c in range(N_CHUNKS)
+        ]
+
+        def load_theta(c):
+            nc.sync.dma_start(out=theta_raw[c][:], in_=theta_rows[:, :, c * CHUNK : (c + 1) * CHUNK])
+
+        nc.sync.dma_start(out=phi_raw[:], in_=phi_rows)
+        load_theta(0)
+        load_theta(1)
+        nc.sync.dma_start(out=g_raw[:], in_=g_rows)
+        load_theta(2)
+        load_theta(3)
+
+        identity = keep.tile([P, P], F32)
+        make_identity(nc, identity[:])
+
+        phi_grouped = keep.tile([P, PACK, P, PACK], BF16, align_bytes=64)
+        phi_codes = keep.tile([P, POOLED], U32, align_bytes=64)
+        phi_scales = keep.tile([P, POOLED], U8, align_bytes=64)
+        g_grouped = keep.tile([P, FEATURES, PACK], BF16, align_bytes=64)
+        g_codes = keep.tile([P, FEATURES], U32, align_bytes=64)
+        g_scales = keep.tile([P, FEATURES], U8, align_bytes=64)
+        theta_grouped = [
+            keep.tile([P, CHUNK, PACK], BF16, align_bytes=64, name="theta_grouped%d" % c)
+            for c in range(N_CHUNKS)
+        ]
+        theta_codes = [
+            keep.tile([P, CHUNK], U32, align_bytes=64, name="theta_codes%d" % c)
+            for c in range(N_CHUNKS)
+        ]
+        theta_scales = [
+            keep.tile([P, CHUNK], U8, align_bytes=64, name="theta_scales%d" % c)
+            for c in range(N_CHUNKS)
+        ]
+        f_grouped = [
+            keep.tile([P, CHUNK, PACK], BF16, align_bytes=64, name="f_grouped%d" % c)
+            for c in range(N_CHUNKS)
+        ]
+        f_codes = [
+            keep.tile([P, CHUNK], U32, align_bytes=64, name="f_codes%d" % c) for c in range(N_CHUNKS)
+        ]
+        f_scales = [
+            keep.tile([P, CHUNK], U8, align_bytes=64, name="f_scales%d" % c) for c in range(N_CHUNKS)
+        ]
+
+        def quantise(grouped, codes, scales):
+            nc.vector.quantize_mx(out=codes[:].bitcast(FP8X4), scales=scales[:], in_=grouped)
+
+        def regroup_phi():
+            nc.vector.tensor_copy(
+                out=phi_grouped[:], in_=phi_raw[:].rearrange("p j (q t) -> p t q j", t=PACK)
+            )
+
+        def regroup_views(c, columns):
+            return (
+                theta_grouped[c][:, columns, :].rearrange("p (w i) j -> p w j i", i=4),
+                theta_raw[c][:, :, columns].rearrange("p j (w i) -> p w j i", i=4),
+            )
+
+        def regroup_theta(c):
+            if c < SHARED_CHUNKS:
+                to_v, from_v = regroup_views(c, slice(0, CHUNK // 2))
+                to_s, from_s = regroup_views(c, slice(CHUNK // 2, CHUNK))
+                nc.vector.tensor_copy(out=to_v, in_=from_v)
+                nc.scalar.copy(out=to_s, in_=from_s)
+            else:
+                to_v, from_v = regroup_views(c, slice(0, CHUNK))
+                nc.vector.tensor_copy(out=to_v, in_=from_v)
+
+        def quantise_theta(c):
+            quantise(
+                theta_grouped[c][:].rearrange("p n j -> p (n j)"), theta_codes[c], theta_scales[c]
+            )
+
+        def first_product(c):
+            for s in range(PACK):
+                columns = slice(s * SUB, (s + 1) * SUB)
+                f_bank = f_banks.tile([P, PACK, SUB], F32)
+                for t in range(PACK):
+                    nc.tensor.matmul_mx(
+                        out=f_bank[:, t, :],
+                        lhsT=phi_codes[:, t * P : (t + 1) * P].bitcast(FP8X4),
+                        lhsT_scale=phi_scales[:, t * P : (t + 1) * P],
+                        rhs=theta_codes[c][:, columns].bitcast(FP8X4),
+                        rhs_scale=theta_scales[c][:, columns],
+                        start=True,
+                        stop=True,
+                    )
+                nc.scalar.activation(
+                    out=f_grouped[c][:, columns, :],
+                    in_=f_bank[:].rearrange("q t n -> q n t"),
+                    func=COPY,
+                    scale=1.0 / POOLED,
+                )
+
+        def quantise_f(c):
+            quantise(f_grouped[c][:].rearrange("q n t -> q (n t)"), f_codes[c], f_scales[c])
+
+        def transpose_g():
+            g_words = g_raw[:].bitcast(F32).rearrange("p b (q u) -> p b u q", u=2)
+            g_grouped_words = g_grouped[:].bitcast(F32)
+            for half in range(2):
+                g_bank = y_banks.tile([P, 2, 2 * P], F32, tag="y_bank")
+                for b in range(2):
+                    for u in range(2):
+                        nc.tensor.transpose(
+                            g_bank[:, u, b * P : (b + 1) * P], g_words[:, 2 * half + b, u, :], identity[:]
+                        )
+                nc.vector.tensor_copy(
+                    out=g_grouped_words[:, half * 2 * P : (half + 1) * 2 * P, :],
+                    in_=g_bank[:].rearrange("q u d -> q d u"),
+                )
+
+        def quantise_g():
+            quantise(g_grouped[:].rearrange("q d t -> q (d t)"), g_codes, g_scales)
+
+        def second_product(c):
+            for b in range(N_BLOCKS):
+                y_bank = y_banks.tile([P, CHUNK], F32, tag="y_bank")
+                nc.tensor.matmul_mx(
+                    out=y_bank[:],
+                    lhsT=g_codes[:, b * P : (b + 1) * P].bitcast(FP8X4),
+                    lhsT_scale=g_scales[:, b * P : (b + 1) * P],
+                    rhs=f_codes[c][:].bitcast(FP8X4),
+                    rhs_scale=f_scales[c][:],
+                    start=True,
+                    stop=True,
+                )
+                y_sb = keep.tile([P, CHUNK], F32, name="y_sb%d_%d" % (c, b))
+                if b % 2 == 0:
+                    nc.vector.tensor_copy(out=y_sb[:], in_=y_bank[:])
+                else:
+                    nc.scalar.copy(out=y_sb[:], in_=y_bank[:])
+                nc.sync.dma_start(out=out_rows[b, :, c * CHUNK : (c + 1) * CHUNK], in_=y_sb[:])
+
+        regroup_phi()
+        regroup_theta(0)
+        quantise(phi_grouped[:].rearrange("p t q j -> p (t q j)"), phi_codes, phi_scales)
+        quantise_theta(0)
+        regroup_theta(1)
+        first_product(0)
+        quantise_theta(1)
+        transpose_g()
+        for c in range(N_CHUNKS):
+            if c + 2 < N_CHUNKS:
+                regroup_theta(c + 2)
+            if c == 0:
+                quantise_g()
+            if c + 1 < N_CHUNKS:
+                first_product(c + 1)
+            quantise_f(c)
+            if c + 2 < N_CHUNKS:
+                quantise_theta(c + 2)
+            second_product(c)

@@ -48,8 +48,8 @@ def tile_nonlocalblocknd_pb_kernel(tc, theta_x, phi_x, g_x, out):
         nc.sync.dma_start(out=phi_raw[:], in_=phi_rows)
         load_theta(0)
         load_theta(1)
-        nc.sync.dma_start(out=g_raw[:], in_=g_rows)
         load_theta(2)
+        nc.sync.dma_start(out=g_raw[:], in_=g_rows)
         load_theta(3)
 
         identity = keep.tile([P, P], F32)
@@ -147,10 +147,12 @@ def tile_nonlocalblocknd_pb_kernel(tc, theta_x, phi_x, g_x, out):
                         nc.tensor.transpose(
                             g_bank[:, u, b * P : (b + 1) * P], g_words[:, 2 * half + b, u, :], identity[:]
                         )
-                nc.vector.tensor_copy(
-                    out=g_grouped_words[:, half * 2 * P : (half + 1) * 2 * P, :],
-                    in_=g_bank[:].rearrange("q u d -> q d u"),
-                )
+                to_words = g_grouped_words[:, half * 2 * P : (half + 1) * 2 * P, :]
+                from_bank = g_bank[:].rearrange("q u d -> q d u")
+                if half % 2 == 0:
+                    nc.vector.tensor_copy(out=to_words, in_=from_bank)
+                else:
+                    nc.scalar.copy(out=to_words, in_=from_bank)
 
         def quantise_g():
             quantise(g_grouped[:].rearrange("q d t -> q (d t)"), g_codes, g_scales)

@@ -19,7 +19,7 @@ CHUNK = 512
 N_CHUNKS = POSITIONS // CHUNK
 SUB = CHUNK // PACK
 N_BLOCKS = FEATURES // P
-SHARED_CHUNKS = 2
+SHARED_CHUNKS = 1
 
 FLOPS = 2 * POSITIONS * POOLED * FEATURES * 2
 
@@ -47,9 +47,9 @@ def tile_nonlocalblocknd_pb_kernel(tc, theta_x, phi_x, g_x, out):
 
         nc.sync.dma_start(out=phi_raw[:], in_=phi_rows)
         load_theta(0)
+        nc.sync.dma_start(out=g_raw[:], in_=g_rows)
         load_theta(1)
         load_theta(2)
-        nc.sync.dma_start(out=g_raw[:], in_=g_rows)
         load_theta(3)
 
         identity = keep.tile([P, P], F32)
@@ -147,12 +147,10 @@ def tile_nonlocalblocknd_pb_kernel(tc, theta_x, phi_x, g_x, out):
                         nc.tensor.transpose(
                             g_bank[:, u, b * P : (b + 1) * P], g_words[:, 2 * half + b, u, :], identity[:]
                         )
-                to_words = g_grouped_words[:, half * 2 * P : (half + 1) * 2 * P, :]
-                from_bank = g_bank[:].rearrange("q u d -> q d u")
-                if half % 2 == 0:
-                    nc.vector.tensor_copy(out=to_words, in_=from_bank)
-                else:
-                    nc.scalar.copy(out=to_words, in_=from_bank)
+                nc.scalar.copy(
+                    out=g_grouped_words[:, half * 2 * P : (half + 1) * 2 * P, :],
+                    in_=g_bank[:].rearrange("q u d -> q d u"),
+                )
 
         def quantise_g():
             quantise(g_grouped[:].rearrange("q d t -> q (d t)"), g_codes, g_scales)
@@ -176,22 +174,24 @@ def tile_nonlocalblocknd_pb_kernel(tc, theta_x, phi_x, g_x, out):
                     nc.scalar.copy(out=y_sb[:], in_=y_bank[:])
                 nc.sync.dma_start(out=out_rows[b, :, c * CHUNK : (c + 1) * CHUNK], in_=y_sb[:])
 
-        regroup_phi()
-        regroup_theta(0)
-        quantise(phi_grouped[:].rearrange("p t q j -> p (t q j)"), phi_codes, phi_scales)
-        quantise_theta(0)
-        regroup_theta(1)
-        first_product(0)
-        quantise_theta(1)
-        transpose_g()
-        for c in range(N_CHUNKS):
-            if c + 2 < N_CHUNKS:
-                regroup_theta(c + 2)
-            if c == 0:
-                quantise_g()
-            if c + 1 < N_CHUNKS:
-                first_product(c + 1)
-            quantise_f(c)
-            if c + 2 < N_CHUNKS:
-                quantise_theta(c + 2)
-            second_product(c)
+        with tc.manual_schedule():
+            regroup_phi()
+            regroup_theta(0)
+            quantise(phi_grouped[:].rearrange("p t q j -> p (t q j)"), phi_codes, phi_scales)
+            quantise_theta(0)
+            transpose_g()
+            first_product(0)
+            regroup_theta(1)
+            quantise_g()
+            quantise_theta(1)
+            regroup_theta(2)
+            first_product(1)
+            for c in range(N_CHUNKS):
+                quantise_f(c)
+                if c + 2 < N_CHUNKS:
+                    quantise_theta(c + 2)
+                if c + 3 < N_CHUNKS:
+                    regroup_theta(c + 3)
+                second_product(c)
+                if c + 2 < N_CHUNKS:
+                    first_product(c + 2)

@@ -15,11 +15,15 @@ PACK = 4
 FEATURES = 512
 POSITIONS = 2048
 POOLED = 512
-CHUNK = 512
+BANK = 512
+LOAD = 512
+N_LOADS = POSITIONS // LOAD
+CHUNK = 256
 N_CHUNKS = POSITIONS // CHUNK
-SUB = CHUNK // PACK
+SUB = BANK // PACK
 N_BLOCKS = FEATURES // P
-SHARED_CHUNKS = 1
+PAIR = BANK // CHUNK
+SHARED_CHUNKS = 2
 
 FLOPS = 2 * POSITIONS * POOLED * FEATURES * 2
 
@@ -29,7 +33,7 @@ def tile_nonlocalblocknd_pb_kernel(tc, theta_x, phi_x, g_x, out):
     theta_rows = theta_x[0].rearrange("(p j) n -> p j n", j=PACK)
     phi_rows = phi_x[0].rearrange("(p j) m -> p j m", j=PACK)
     g_rows = g_x[0].rearrange("(b p) m -> p b m", p=P)
-    out_rows = out[0].rearrange("(b p) n -> b p n", p=P)
+    out_rows = out[0].rearrange("(h b p) n -> h p b n", b=PAIR, p=P)
 
     with ExitStack() as ctx:
         keep = ctx.enter_context(tc.tile_pool(name="keep", bufs=1))
@@ -39,18 +43,17 @@ def tile_nonlocalblocknd_pb_kernel(tc, theta_x, phi_x, g_x, out):
         phi_raw = keep.tile([P, PACK, POOLED], BF16)
         g_raw = keep.tile([P, N_BLOCKS, POOLED], BF16)
         theta_raw = [
-            keep.tile([P, PACK, CHUNK], BF16, name="theta_raw%d" % c) for c in range(N_CHUNKS)
+            keep.tile([P, PACK, LOAD], BF16, name="theta_raw%d" % i) for i in range(N_LOADS)
         ]
 
-        def load_theta(c):
-            nc.sync.dma_start(out=theta_raw[c][:], in_=theta_rows[:, :, c * CHUNK : (c + 1) * CHUNK])
+        def load_theta(i):
+            nc.sync.dma_start(out=theta_raw[i][:], in_=theta_rows[:, :, i * LOAD : (i + 1) * LOAD])
 
         nc.sync.dma_start(out=phi_raw[:], in_=phi_rows)
         load_theta(0)
         nc.sync.dma_start(out=g_raw[:], in_=g_rows)
-        load_theta(1)
-        load_theta(2)
-        load_theta(3)
+        for i in range(1, N_LOADS):
+            load_theta(i)
 
         identity = keep.tile([P, P], F32)
         make_identity(nc, identity[:])
@@ -83,6 +86,9 @@ def tile_nonlocalblocknd_pb_kernel(tc, theta_x, phi_x, g_x, out):
         f_scales = [
             keep.tile([P, CHUNK], U8, align_bytes=64, name="f_scales%d" % c) for c in range(N_CHUNKS)
         ]
+        g_filled = []
+        f_filled = []
+        y_filled = []
 
         def quantise(grouped, codes, scales):
             nc.vector.quantize_mx(out=codes[:].bitcast(FP8X4), scales=scales[:], in_=grouped)
@@ -92,20 +98,25 @@ def tile_nonlocalblocknd_pb_kernel(tc, theta_x, phi_x, g_x, out):
                 out=phi_grouped[:], in_=phi_raw[:].rearrange("p j (q t) -> p t q j", t=PACK)
             )
 
-        def regroup_views(c, columns):
+        def quantise_phi():
+            quantise(phi_grouped[:].rearrange("p t q j -> p (t q j)"), phi_codes, phi_scales)
+
+        def regroup_views(c, start, stop):
+            raw = theta_raw[c * CHUNK // LOAD]
+            first = c * CHUNK % LOAD
             return (
-                theta_grouped[c][:, columns, :].rearrange("p (w i) j -> p w j i", i=4),
-                theta_raw[c][:, :, columns].rearrange("p j (w i) -> p w j i", i=4),
+                theta_grouped[c][:, start:stop, :].rearrange("p (w i) j -> p w j i", i=4),
+                raw[:, :, first + start : first + stop].rearrange("p j (w i) -> p w j i", i=4),
             )
 
         def regroup_theta(c):
             if c < SHARED_CHUNKS:
-                to_v, from_v = regroup_views(c, slice(0, CHUNK // 2))
-                to_s, from_s = regroup_views(c, slice(CHUNK // 2, CHUNK))
+                to_v, from_v = regroup_views(c, 0, CHUNK // 2)
+                to_s, from_s = regroup_views(c, CHUNK // 2, CHUNK)
                 nc.vector.tensor_copy(out=to_v, in_=from_v)
                 nc.scalar.copy(out=to_s, in_=from_s)
             else:
-                to_v, from_v = regroup_views(c, slice(0, CHUNK))
+                to_v, from_v = regroup_views(c, 0, CHUNK)
                 nc.vector.tensor_copy(out=to_v, in_=from_v)
 
         def quantise_theta(c):
@@ -114,7 +125,7 @@ def tile_nonlocalblocknd_pb_kernel(tc, theta_x, phi_x, g_x, out):
             )
 
         def first_product(c):
-            for s in range(PACK):
+            for s in range(CHUNK // SUB):
                 columns = slice(s * SUB, (s + 1) * SUB)
                 f_bank = f_banks.tile([P, PACK, SUB], F32)
                 for t in range(PACK):
@@ -127,8 +138,13 @@ def tile_nonlocalblocknd_pb_kernel(tc, theta_x, phi_x, g_x, out):
                         start=True,
                         stop=True,
                     )
+                f_filled.append(f_bank)
+
+        def empty_f(c):
+            for s in range(CHUNK // SUB):
+                f_bank = f_filled.pop(0)
                 nc.scalar.activation(
-                    out=f_grouped[c][:, columns, :],
+                    out=f_grouped[c][:, s * SUB : (s + 1) * SUB, :],
                     in_=f_bank[:].rearrange("q t n -> q n t"),
                     func=COPY,
                     scale=1.0 / POOLED,
@@ -139,7 +155,6 @@ def tile_nonlocalblocknd_pb_kernel(tc, theta_x, phi_x, g_x, out):
 
         def transpose_g():
             g_words = g_raw[:].bitcast(F32).rearrange("p b (q u) -> p b u q", u=2)
-            g_grouped_words = g_grouped[:].bitcast(F32)
             for half in range(2):
                 g_bank = y_banks.tile([P, 2, 2 * P], F32, tag="y_bank")
                 for b in range(2):
@@ -147,6 +162,12 @@ def tile_nonlocalblocknd_pb_kernel(tc, theta_x, phi_x, g_x, out):
                         nc.tensor.transpose(
                             g_bank[:, u, b * P : (b + 1) * P], g_words[:, 2 * half + b, u, :], identity[:]
                         )
+                g_filled.append(g_bank)
+
+        def empty_g():
+            g_grouped_words = g_grouped[:].bitcast(F32)
+            for half in range(2):
+                g_bank = g_filled.pop(0)
                 nc.scalar.copy(
                     out=g_grouped_words[:, half * 2 * P : (half + 1) * 2 * P, :],
                     in_=g_bank[:].rearrange("q u d -> q d u"),
@@ -156,42 +177,57 @@ def tile_nonlocalblocknd_pb_kernel(tc, theta_x, phi_x, g_x, out):
             quantise(g_grouped[:].rearrange("q d t -> q (d t)"), g_codes, g_scales)
 
         def second_product(c):
-            for b in range(N_BLOCKS):
-                y_bank = y_banks.tile([P, CHUNK], F32, tag="y_bank")
-                nc.tensor.matmul_mx(
-                    out=y_bank[:],
-                    lhsT=g_codes[:, b * P : (b + 1) * P].bitcast(FP8X4),
-                    lhsT_scale=g_scales[:, b * P : (b + 1) * P],
-                    rhs=f_codes[c][:].bitcast(FP8X4),
-                    rhs_scale=f_scales[c][:],
-                    start=True,
-                    stop=True,
-                )
-                y_sb = keep.tile([P, CHUNK], F32, name="y_sb%d_%d" % (c, b))
-                if b % 2 == 0:
+            for h in range(N_BLOCKS // PAIR):
+                y_bank = y_banks.tile([P, PAIR, CHUNK], F32, tag="y_bank")
+                for b in range(PAIR):
+                    rows = slice((h * PAIR + b) * P, (h * PAIR + b + 1) * P)
+                    nc.tensor.matmul_mx(
+                        out=y_bank[:, b, :],
+                        lhsT=g_codes[:, rows].bitcast(FP8X4),
+                        lhsT_scale=g_scales[:, rows],
+                        rhs=f_codes[c][:].bitcast(FP8X4),
+                        rhs_scale=f_scales[c][:],
+                        start=True,
+                        stop=True,
+                    )
+                y_filled.append(y_bank)
+
+        def empty_and_store_y(c):
+            for h in range(N_BLOCKS // PAIR):
+                y_bank = y_filled.pop(0)
+                y_sb = keep.tile([P, PAIR, CHUNK], F32, name="y_sb%d_%d" % (c, h))
+                if h % 2 == 0:
                     nc.vector.tensor_copy(out=y_sb[:], in_=y_bank[:])
                 else:
                     nc.scalar.copy(out=y_sb[:], in_=y_bank[:])
-                nc.sync.dma_start(out=out_rows[b, :, c * CHUNK : (c + 1) * CHUNK], in_=y_sb[:])
+                nc.sync.dma_start(out=out_rows[h, :, :, c * CHUNK : (c + 1) * CHUNK], in_=y_sb[:])
+
+        def live(c):
+            return 0 <= c < N_CHUNKS
 
         with tc.manual_schedule():
             regroup_phi()
             regroup_theta(0)
-            quantise(phi_grouped[:].rearrange("p t q j -> p (t q j)"), phi_codes, phi_scales)
+            quantise_phi()
             quantise_theta(0)
-            transpose_g()
-            first_product(0)
-            regroup_theta(1)
-            quantise_g()
-            quantise_theta(1)
-            regroup_theta(2)
-            first_product(1)
-            for c in range(N_CHUNKS):
-                quantise_f(c)
-                if c + 2 < N_CHUNKS:
-                    quantise_theta(c + 2)
-                if c + 3 < N_CHUNKS:
-                    regroup_theta(c + 3)
-                second_product(c)
-                if c + 2 < N_CHUNKS:
-                    first_product(c + 2)
+            for step in range(N_CHUNKS + 3):
+                if step == 0:
+                    transpose_g()
+                if step == 1:
+                    empty_g()
+                if step == 2:
+                    quantise_g()
+                if live(step + 1):
+                    regroup_theta(step + 1)
+                if live(step - 2):
+                    quantise_f(step - 2)
+                if live(step + 1):
+                    quantise_theta(step + 1)
+                if live(step):
+                    first_product(step)
+                if live(step - 1):
+                    empty_f(step - 1)
+                if live(step - 2):
+                    second_product(step - 2)
+                if live(step - 3):
+                    empty_and_store_y(step - 3)

@@ -16,8 +16,7 @@ FEATURES = 512
 POSITIONS = 2048
 POOLED = 512
 BANK = 512
-LOAD = 512
-N_LOADS = POSITIONS // LOAD
+LOADS = (512, 512, 1024)
 CHUNK = 256
 N_CHUNKS = POSITIONS // CHUNK
 SUB = BANK // PACK
@@ -32,8 +31,8 @@ def tile_nonlocalblocknd_pb_kernel(tc, theta_x, phi_x, g_x, out):
     nc = tc.nc
     theta_rows = theta_x[0].rearrange("(p j) n -> p j n", j=PACK)
     phi_rows = phi_x[0].rearrange("(p j) m -> p j m", j=PACK)
-    g_rows = g_x[0].rearrange("(b p) m -> p b m", p=P)
-    out_rows = out[0].rearrange("(h b p) n -> h p b n", b=PAIR, p=P)
+    g_rows = g_x[0].rearrange("(p b) m -> p b m", b=N_BLOCKS)
+    out_rows = out[0].rearrange("(p h b) n -> h p b n", h=N_BLOCKS // PAIR, b=PAIR)
 
     with ExitStack() as ctx:
         keep = ctx.enter_context(tc.tile_pool(name="keep", bufs=1))
@@ -43,16 +42,24 @@ def tile_nonlocalblocknd_pb_kernel(tc, theta_x, phi_x, g_x, out):
         phi_raw = keep.tile([P, PACK, POOLED], BF16)
         g_raw = keep.tile([P, N_BLOCKS, POOLED], BF16)
         theta_raw = [
-            keep.tile([P, PACK, LOAD], BF16, name="theta_raw%d" % i) for i in range(N_LOADS)
+            keep.tile([P, PACK, width], BF16, name="theta_raw%d" % i)
+            for i, width in enumerate(LOADS)
         ]
+        load_of = {}
+        for i, width in enumerate(LOADS):
+            for first in range(0, width, CHUNK):
+                load_of[len(load_of)] = (i, first)
 
         def load_theta(i):
-            nc.sync.dma_start(out=theta_raw[i][:], in_=theta_rows[:, :, i * LOAD : (i + 1) * LOAD])
+            start = sum(LOADS[:i])
+            nc.sync.dma_start(
+                out=theta_raw[i][:], in_=theta_rows[:, :, start : start + LOADS[i]]
+            )
 
         nc.sync.dma_start(out=phi_raw[:], in_=phi_rows)
         load_theta(0)
         nc.sync.dma_start(out=g_raw[:], in_=g_rows)
-        for i in range(1, N_LOADS):
+        for i in range(1, len(LOADS)):
             load_theta(i)
 
         identity = keep.tile([P, P], F32)
@@ -102,8 +109,8 @@ def tile_nonlocalblocknd_pb_kernel(tc, theta_x, phi_x, g_x, out):
             quantise(phi_grouped[:].rearrange("p t q j -> p (t q j)"), phi_codes, phi_scales)
 
         def regroup_views(c, start, stop):
-            raw = theta_raw[c * CHUNK // LOAD]
-            first = c * CHUNK % LOAD
+            load, first = load_of[c]
+            raw = theta_raw[load]
             return (
                 theta_grouped[c][:, start:stop, :].rearrange("p (w i) j -> p w j i", i=4),
                 raw[:, :, first + start : first + stop].rearrange("p j (w i) -> p w j i", i=4),

@@ -16,13 +16,15 @@ FEATURES = 512
 POSITIONS = 2048
 POOLED = 512
 BANK = 512
-LOADS = (512, 512, 1024)
-CHUNK = 256
-N_CHUNKS = POSITIONS // CHUNK
+LOADS = (256, 256, 512, 1024)
+G_AFTER = 1
+CHUNKS = (256,) * 7 + (128,) * 2
+N_CHUNKS = len(CHUNKS)
+STARTS = [sum(CHUNKS[:c]) for c in range(N_CHUNKS)]
 SUB = BANK // PACK
 N_BLOCKS = FEATURES // P
-PAIR = BANK // CHUNK
-SHARED_CHUNKS = 2
+PAIR = 2
+SCALAR_SHARE = {0: 256, 1: 64, 2: 64}
 
 FLOPS = 2 * POSITIONS * POOLED * FEATURES * 2
 
@@ -45,120 +47,107 @@ def tile_nonlocalblocknd_pb_kernel(tc, theta_x, phi_x, g_x, out):
             keep.tile([P, PACK, width], BF16, name="theta_raw%d" % i)
             for i, width in enumerate(LOADS)
         ]
-        load_of = {}
-        for i, width in enumerate(LOADS):
-            for first in range(0, width, CHUNK):
-                load_of[len(load_of)] = (i, first)
-
-        def load_theta(i):
-            start = sum(LOADS[:i])
-            nc.sync.dma_start(
-                out=theta_raw[i][:], in_=theta_rows[:, :, start : start + LOADS[i]]
-            )
-
         nc.sync.dma_start(out=phi_raw[:], in_=phi_rows)
-        load_theta(0)
-        nc.sync.dma_start(out=g_raw[:], in_=g_rows)
-        for i in range(1, len(LOADS)):
-            load_theta(i)
+        for i, width in enumerate(LOADS):
+            if i == G_AFTER:
+                nc.sync.dma_start(out=g_raw[:], in_=g_rows)
+            start = sum(LOADS[:i])
+            nc.sync.dma_start(out=theta_raw[i][:], in_=theta_rows[:, :, start : start + width])
 
         identity = keep.tile([P, P], F32)
         make_identity(nc, identity[:])
 
-        phi_grouped = keep.tile([P, PACK, P, PACK], BF16, align_bytes=64)
-        phi_codes = keep.tile([P, POOLED], U32, align_bytes=64)
-        phi_scales = keep.tile([P, POOLED], U8, align_bytes=64)
-        g_grouped = keep.tile([P, FEATURES, PACK], BF16, align_bytes=64)
-        g_codes = keep.tile([P, FEATURES], U32, align_bytes=64)
-        g_scales = keep.tile([P, FEATURES], U8, align_bytes=64)
-        theta_grouped = [
-            keep.tile([P, CHUNK, PACK], BF16, align_bytes=64, name="theta_grouped%d" % c)
-            for c in range(N_CHUNKS)
-        ]
-        theta_codes = [
-            keep.tile([P, CHUNK], U32, align_bytes=64, name="theta_codes%d" % c)
-            for c in range(N_CHUNKS)
-        ]
-        theta_scales = [
-            keep.tile([P, CHUNK], U8, align_bytes=64, name="theta_scales%d" % c)
-            for c in range(N_CHUNKS)
-        ]
-        f_grouped = [
-            keep.tile([P, CHUNK, PACK], BF16, align_bytes=64, name="f_grouped%d" % c)
-            for c in range(N_CHUNKS)
-        ]
-        f_codes = [
-            keep.tile([P, CHUNK], U32, align_bytes=64, name="f_codes%d" % c) for c in range(N_CHUNKS)
-        ]
-        f_scales = [
-            keep.tile([P, CHUNK], U8, align_bytes=64, name="f_scales%d" % c) for c in range(N_CHUNKS)
-        ]
-        g_filled = []
-        f_filled = []
-        y_filled = []
-
-        def quantise(grouped, codes, scales):
-            nc.vector.quantize_mx(out=codes[:].bitcast(FP8X4), scales=scales[:], in_=grouped)
-
-        def regroup_phi():
-            nc.vector.tensor_copy(
-                out=phi_grouped[:], in_=phi_raw[:].rearrange("p j (q t) -> p t q j", t=PACK)
+        def operand(columns, name):
+            return (
+                keep.tile([P, columns, PACK], BF16, align_bytes=64, name=name + "_grouped"),
+                keep.tile([P, columns], U32, align_bytes=64, name=name + "_codes"),
+                keep.tile([P, columns], U8, align_bytes=64, name=name + "_scales"),
             )
 
-        def quantise_phi():
-            quantise(phi_grouped[:].rearrange("p t q j -> p (t q j)"), phi_codes, phi_scales)
+        phi_grouped, phi_codes, phi_scales = operand(POOLED, "phi")
+        g_grouped, g_codes, g_scales = operand(FEATURES, "g")
+        theta = [operand(width, "theta%d" % c) for c, width in enumerate(CHUNKS)]
+        f = [operand(width, "f%d" % c) for c, width in enumerate(CHUNKS)]
+        g_filled = {}
+        f_filled = {}
+        y_filled = {}
+
+        def copy(engine, to, source):
+            if engine == "V":
+                nc.vector.tensor_copy(out=to, in_=source)
+            else:
+                nc.scalar.copy(out=to, in_=source)
+
+        def quantise(operand_tiles, start, stop):
+            grouped, codes, scales = operand_tiles
+            nc.vector.quantize_mx(
+                out=codes[:, start:stop].bitcast(FP8X4),
+                scales=scales[:, start:stop],
+                in_=grouped[:].rearrange("p c j -> p (c j)")[:, start * PACK : stop * PACK],
+            )
+
+        def regroup_phi(engine, start, stop):
+            for_t = slice(start, stop)
+            copy(
+                engine,
+                phi_grouped[:].rearrange("p (t q) j -> p t q j", t=PACK)[:, for_t],
+                phi_raw[:].rearrange("p j (q t) -> p t q j", t=PACK)[:, for_t],
+            )
+
+        def quantise_phi(half):
+            quantise((phi_grouped, phi_codes, phi_scales), half * 2 * P, (half + 1) * 2 * P)
 
         def regroup_views(c, start, stop):
-            load, first = load_of[c]
-            raw = theta_raw[load]
+            load = 0
+            first = STARTS[c]
+            while first >= LOADS[load]:
+                first -= LOADS[load]
+                load += 1
             return (
-                theta_grouped[c][:, start:stop, :].rearrange("p (w i) j -> p w j i", i=4),
-                raw[:, :, first + start : first + stop].rearrange("p j (w i) -> p w j i", i=4),
+                theta[c][0][:, start:stop, :].rearrange("p (w i) j -> p w j i", i=4),
+                theta_raw[load][:, :, first + start : first + stop].rearrange(
+                    "p j (w i) -> p w j i", i=4
+                ),
             )
 
         def regroup_theta(c):
-            if c < SHARED_CHUNKS:
-                to_v, from_v = regroup_views(c, 0, CHUNK // 2)
-                to_s, from_s = regroup_views(c, CHUNK // 2, CHUNK)
-                nc.vector.tensor_copy(out=to_v, in_=from_v)
-                nc.scalar.copy(out=to_s, in_=from_s)
-            else:
-                to_v, from_v = regroup_views(c, 0, CHUNK)
-                nc.vector.tensor_copy(out=to_v, in_=from_v)
+            scalar = SCALAR_SHARE.get(c, 0)
+            if scalar:
+                copy("S", *regroup_views(c, 0, scalar))
+            if scalar < CHUNKS[c]:
+                copy("V", *regroup_views(c, scalar, CHUNKS[c]))
 
         def quantise_theta(c):
-            quantise(
-                theta_grouped[c][:].rearrange("p n j -> p (n j)"), theta_codes[c], theta_scales[c]
-            )
+            quantise(theta[c], 0, CHUNKS[c])
 
         def first_product(c):
-            for s in range(CHUNK // SUB):
+            for s in range(CHUNKS[c] // SUB):
                 columns = slice(s * SUB, (s + 1) * SUB)
-                f_bank = f_banks.tile([P, PACK, SUB], F32)
+                f_bank = f_banks.tile([P, PACK, SUB], F32, tag="f_bank")
                 for t in range(PACK):
                     nc.tensor.matmul_mx(
                         out=f_bank[:, t, :],
                         lhsT=phi_codes[:, t * P : (t + 1) * P].bitcast(FP8X4),
                         lhsT_scale=phi_scales[:, t * P : (t + 1) * P],
-                        rhs=theta_codes[c][:, columns].bitcast(FP8X4),
-                        rhs_scale=theta_scales[c][:, columns],
+                        rhs=theta[c][1][:, columns].bitcast(FP8X4),
+                        rhs_scale=theta[c][2][:, columns],
                         start=True,
                         stop=True,
                     )
-                f_filled.append(f_bank)
+                f_filled[c, s] = f_bank
 
-        def empty_f(c):
-            for s in range(CHUNK // SUB):
-                f_bank = f_filled.pop(0)
-                nc.scalar.activation(
-                    out=f_grouped[c][:, s * SUB : (s + 1) * SUB, :],
-                    in_=f_bank[:].rearrange("q t n -> q n t"),
-                    func=COPY,
-                    scale=1.0 / POOLED,
-                )
+        def empty_f(c, s):
+            if s >= CHUNKS[c] // SUB:
+                return
+            to = f[c][0][:, s * SUB : (s + 1) * SUB, :]
+            source = f_filled[c, s][:].rearrange("q t n -> q n t")
+            if f_engine(c, s) == "V":
+                nc.vector.tensor_scalar_mul(to, source, 1.0 / POOLED)
+            else:
+                nc.scalar.activation(out=to, in_=source, func=COPY, scale=1.0 / POOLED)
 
         def quantise_f(c):
-            quantise(f_grouped[c][:].rearrange("q n t -> q (n t)"), f_codes[c], f_scales[c])
+            quantise(f[c], 0, CHUNKS[c])
 
         def transpose_g():
             g_words = g_raw[:].bitcast(F32).rearrange("p b (q u) -> p b u q", u=2)
@@ -169,72 +158,83 @@ def tile_nonlocalblocknd_pb_kernel(tc, theta_x, phi_x, g_x, out):
                         nc.tensor.transpose(
                             g_bank[:, u, b * P : (b + 1) * P], g_words[:, 2 * half + b, u, :], identity[:]
                         )
-                g_filled.append(g_bank)
+                g_filled[half] = g_bank
 
-        def empty_g():
-            g_grouped_words = g_grouped[:].bitcast(F32)
-            for half in range(2):
-                g_bank = g_filled.pop(0)
-                nc.scalar.copy(
-                    out=g_grouped_words[:, half * 2 * P : (half + 1) * 2 * P, :],
-                    in_=g_bank[:].rearrange("q u d -> q d u"),
-                )
+        def empty_g(engine, half):
+            columns = slice(half * 2 * P, (half + 1) * 2 * P)
+            copy(
+                engine,
+                g_grouped[:].bitcast(F32)[:, columns, :],
+                g_filled[half][:].rearrange("q u d -> q d u"),
+            )
 
         def quantise_g():
-            quantise(g_grouped[:].rearrange("q d t -> q (d t)"), g_codes, g_scales)
+            quantise((g_grouped, g_codes, g_scales), 0, FEATURES)
 
         def second_product(c):
             for h in range(N_BLOCKS // PAIR):
-                y_bank = y_banks.tile([P, PAIR, CHUNK], F32, tag="y_bank")
+                y_bank = y_banks.tile([P, PAIR, CHUNKS[c]], F32, tag="y_bank")
                 for b in range(PAIR):
                     rows = slice((h * PAIR + b) * P, (h * PAIR + b + 1) * P)
                     nc.tensor.matmul_mx(
                         out=y_bank[:, b, :],
                         lhsT=g_codes[:, rows].bitcast(FP8X4),
                         lhsT_scale=g_scales[:, rows],
-                        rhs=f_codes[c][:].bitcast(FP8X4),
-                        rhs_scale=f_scales[c][:],
+                        rhs=f[c][1][:].bitcast(FP8X4),
+                        rhs_scale=f[c][2][:],
                         start=True,
                         stop=True,
                     )
-                y_filled.append(y_bank)
+                y_filled[c, h] = y_bank
 
-        def empty_and_store_y(c):
-            for h in range(N_BLOCKS // PAIR):
-                y_bank = y_filled.pop(0)
-                y_sb = keep.tile([P, PAIR, CHUNK], F32, name="y_sb%d_%d" % (c, h))
-                if h % 2 == 0:
-                    nc.vector.tensor_copy(out=y_sb[:], in_=y_bank[:])
-                else:
-                    nc.scalar.copy(out=y_sb[:], in_=y_bank[:])
-                nc.sync.dma_start(out=out_rows[h, :, :, c * CHUNK : (c + 1) * CHUNK], in_=y_sb[:])
+        def empty_y(c, h):
+            y_sb = keep.tile([P, PAIR, CHUNKS[c]], F32, name="y_sb%d_%d" % (c, h))
+            copy(y_engine(c, h), y_sb[:], y_filled[c, h][:])
+            nc.sync.dma_start(
+                out=out_rows[h, :, :, STARTS[c] : STARTS[c] + CHUNKS[c]], in_=y_sb[:]
+            )
 
         def live(c):
             return 0 <= c < N_CHUNKS
 
+        def f_engine(c, s):
+            if c < 2 or c == N_CHUNKS - 1:
+                return "S"
+            return "VS"[s]
+
+        def y_engine(c, h):
+            return "V" if (c, h) in ((N_CHUNKS - 3, 1), (N_CHUNKS - 1, 0)) else "S"
+
         with tc.manual_schedule():
-            regroup_phi()
+            regroup_phi("V", 0, 2)
+            regroup_phi("S", 2, 3)
+            regroup_phi("V", 3, 4)
+            transpose_g()
             regroup_theta(0)
-            quantise_phi()
+            quantise_phi(0)
+            quantise_phi(1)
             quantise_theta(0)
-            for step in range(N_CHUNKS + 3):
-                if step == 0:
-                    transpose_g()
-                if step == 1:
-                    empty_g()
-                if step == 2:
+            first_product(0)
+            regroup_theta(1)
+            empty_g("S", 0)
+            empty_g("V", 1)
+            for c in range(N_CHUNKS + 1):
+                if live(c + 1):
+                    quantise_theta(c + 1)
+                if live(c):
+                    empty_f(c, 0)
+                    empty_f(c, 1)
+                if live(c - 1):
+                    empty_y(c - 1, 0)
+                if live(c + 1):
+                    first_product(c + 1)
+                if live(c + 2):
+                    regroup_theta(c + 2)
+                if c == 0:
                     quantise_g()
-                if live(step + 1):
-                    regroup_theta(step + 1)
-                if live(step - 2):
-                    quantise_f(step - 2)
-                if live(step + 1):
-                    quantise_theta(step + 1)
-                if live(step):
-                    first_product(step)
-                if live(step - 1):
-                    empty_f(step - 1)
-                if live(step - 2):
-                    second_product(step - 2)
-                if live(step - 3):
-                    empty_and_store_y(step - 3)
+                if live(c):
+                    quantise_f(c)
+                if live(c - 1):
+                    empty_y(c - 1, 1)
+                if live(c):
+                    second_product(c)

@@ -25,6 +25,7 @@ SUB = BANK // PACK
 N_BLOCKS = FEATURES // P
 PAIR = 2
 SCALAR_SHARE = {0: 256, 1: 64, 2: 64}
+HOP = 8
 
 FLOPS = 2 * POSITIONS * POOLED * FEATURES * 2
 
@@ -104,9 +105,9 @@ def tile_nonlocalblocknd_pb_kernel(tc, theta_x, phi_x, g_x, out):
                 first -= LOADS[load]
                 load += 1
             return (
-                theta[c][0][:, start:stop, :].rearrange("p (w i) j -> p w j i", i=4),
+                theta[c][0][:, start:stop, :].rearrange("p (w i) j -> p w j i", i=HOP),
                 theta_raw[load][:, :, first + start : first + stop].rearrange(
-                    "p j (w i) -> p w j i", i=4
+                    "p j (w i) -> p w j i", i=HOP
                 ),
             )
 

@@ -26,6 +26,8 @@ N_BLOCKS = FEATURES // P
 PAIR = 2
 SCALAR_SHARE = {0: 256, 1: 64, 2: 64}
 HOP = 8
+WARM_ZEROS = 6
+WARM_PHI = PACK
 
 FLOPS = 2 * POSITIONS * POOLED * FEATURES * 2
 
@@ -55,6 +57,8 @@ def tile_nonlocalblocknd_pb_kernel(tc, theta_x, phi_x, g_x, out):
             start = sum(LOADS[:i])
             nc.sync.dma_start(out=theta_raw[i][:], in_=theta_rows[:, :, start : start + width])
 
+        zeros = keep.tile([P, BANK], BF16)
+        nc.vector.memset(zeros[:], 0.0)
         identity = keep.tile([P, P], F32)
         make_identity(nc, identity[:])
 
@@ -198,6 +202,12 @@ def tile_nonlocalblocknd_pb_kernel(tc, theta_x, phi_x, g_x, out):
         def live(c):
             return 0 <= c < N_CHUNKS
 
+        def warm_up():
+            warm_bank = f_banks.tile([P, BANK], F32, tag="f_bank")
+            moving = [zeros[:]] * WARM_ZEROS + [phi_raw[:, j, :] for j in range(WARM_PHI)]
+            for rhs in moving:
+                nc.tensor.matmul(warm_bank[:], lhsT=zeros[:, :P], rhs=rhs, start=True, stop=True)
+
         def f_engine(c, s):
             if c < 2 or c == N_CHUNKS - 1:
                 return "S"
@@ -207,6 +217,7 @@ def tile_nonlocalblocknd_pb_kernel(tc, theta_x, phi_x, g_x, out):
             return "V" if (c, h) in ((N_CHUNKS - 3, 1), (N_CHUNKS - 1, 0)) else "S"
 
         with tc.manual_schedule():
+            warm_up()
             regroup_phi("V", 0, 2)
             regroup_phi("S", 2, 3)
             regroup_phi("V", 3, 4)

@@ -24,7 +24,7 @@ STARTS = [sum(CHUNKS[:c]) for c in range(N_CHUNKS)]
 SUB = BANK // PACK
 N_BLOCKS = FEATURES // P
 PAIR = 2
-SCALAR_SHARE = {0: 256, 1: 64, 2: 64}
+SCALAR_SHARE = {0: 128, 1: 64, 2: 64}
 HOP = 8
 WARM_ZEROS = 6
 WARM_PHI = PACK
@@ -214,7 +214,7 @@ def tile_nonlocalblocknd_pb_kernel(tc, theta_x, phi_x, g_x, out):
             return "VS"[s]
 
         def y_engine(c, h):
-            return "V" if (c, h) in ((N_CHUNKS - 3, 1), (N_CHUNKS - 1, 0)) else "S"
+            return "V" if (c, h) in ((N_CHUNKS - 3, 1), (N_CHUNKS - 1, 1)) else "S"
 
         with tc.manual_schedule():
             warm_up()

from contextlib import ExitStack

import concourse.mybir as mybir
from concourse.masks import make_identity

BF16 = mybir.dt.bfloat16
F32 = mybir.dt.float32
U32 = mybir.dt.uint32
U8 = mybir.dt.uint8
FP8X4 = mybir.dt.float8_e4m3fn_x4
COPY = mybir.ActivationFunctionType.Copy

P = 128
PACK = 4
FEATURES = 512
POSITIONS = 2048
POOLED = 512
BANK = 512
LOADS = (256, 256, 512, 1024)
G_AFTER = 1
CHUNKS = (256,) * 7 + (128,) * 2
N_CHUNKS = len(CHUNKS)
STARTS = [sum(CHUNKS[:c]) for c in range(N_CHUNKS)]
SUB = BANK // PACK
N_BLOCKS = FEATURES // P
PAIR = 2
SCALAR_SHARE = {0: 128, 1: 64, 2: 64}
HOP = 8
WARM_ZEROS = 6
WARM_PHI = PACK

FLOPS = 2 * POSITIONS * POOLED * FEATURES * 2


def tile_nonlocalblocknd_pb_kernel(tc, theta_x, phi_x, g_x, out):
    nc = tc.nc
    theta_rows = theta_x[0].rearrange("(p j) n -> p j n", j=PACK)
    phi_rows = phi_x[0].rearrange("(p j) m -> p j m", j=PACK)
    g_rows = g_x[0].rearrange("(p b) m -> p b m", b=N_BLOCKS)
    out_rows = out[0].rearrange("(p h b) n -> h p b n", h=N_BLOCKS // PAIR, b=PAIR)

    with ExitStack() as ctx:
        keep = ctx.enter_context(tc.tile_pool(name="keep", bufs=1))
        f_banks = ctx.enter_context(tc.psum_pool(name="f_banks", bufs=4))
        y_banks = ctx.enter_context(tc.psum_pool(name="y_banks", bufs=4))

        phi_raw = keep.tile([P, PACK, POOLED], BF16)
        g_raw = keep.tile([P, N_BLOCKS, POOLED], BF16)
        theta_raw = [
            keep.tile([P, PACK, width], BF16, name="theta_raw%d" % i)
            for i, width in enumerate(LOADS)
        ]
        nc.sync.dma_start(out=phi_raw[:], in_=phi_rows)
        for i, width in enumerate(LOADS):
            if i == G_AFTER:
                nc.sync.dma_start(out=g_raw[:], in_=g_rows)
            start = sum(LOADS[:i])
            nc.sync.dma_start(out=theta_raw[i][:], in_=theta_rows[:, :, start : start + width])

        zeros = keep.tile([P, BANK], BF16)
        nc.vector.memset(zeros[:], 0.0)
        identity = keep.tile([P, P], F32)
        make_identity(nc, identity[:])

        def operand(columns, name):
            return (
                keep.tile([P, columns, PACK], BF16, align_bytes=64, name=name + "_grouped"),
                keep.tile([P, columns], U32, align_bytes=64, name=name + "_codes"),
                keep.tile([P, columns], U8, align_bytes=64, name=name + "_scales"),
            )

        phi_grouped, phi_codes, phi_scales = operand(POOLED, "phi")
        g_grouped, g_codes, g_scales = operand(FEATURES, "g")
        theta = [operand(width, "theta%d" % c) for c, width in enumerate(CHUNKS)]
        f = [operand(width, "f%d" % c) for c, width in enumerate(CHUNKS)]
        g_filled = {}
        f_filled = {}
        y_filled = {}

        def copy(engine, to, source):
            if engine == "V":
                nc.vector.tensor_copy(out=to, in_=source)
            else:
                nc.scalar.copy(out=to, in_=source)

        def quantise(operand_tiles, start, stop):
            grouped, codes, scales = operand_tiles
            nc.vector.quantize_mx(
                out=codes[:, start:stop].bitcast(FP8X4),
                scales=scales[:, start:stop],
                in_=grouped[:].rearrange("p c j -> p (c j)")[:, start * PACK : stop * PACK],
            )

        def regroup_phi(engine, start, stop):
            for_t = slice(start, stop)
            copy(
                engine,
                phi_grouped[:].rearrange("p (t q) j -> p t q j", t=PACK)[:, for_t],
                phi_raw[:].rearrange("p j (q t) -> p t q j", t=PACK)[:, for_t],
            )

        def quantise_phi(half):
            quantise((phi_grouped, phi_codes, phi_scales), half * 2 * P, (half + 1) * 2 * P)

        def regroup_views(c, start, stop):
            load = 0
            first = STARTS[c]
            while first >= LOADS[load]:
                first -= LOADS[load]
                load += 1
            return (
                theta[c][0][:, start:stop, :].rearrange("p (w i) j -> p w j i", i=HOP),
                theta_raw[load][:, :, first + start : first + stop].rearrange(
                    "p j (w i) -> p w j i", i=HOP
                ),
            )

        def regroup_theta(c):
            scalar = SCALAR_SHARE.get(c, 0)
            if scalar:
                copy("S", *regroup_views(c, 0, scalar))
            if scalar < CHUNKS[c]:
                copy("V", *regroup_views(c, scalar, CHUNKS[c]))

        def quantise_theta(c):
            quantise(theta[c], 0, CHUNKS[c])

        def first_product(c):
            for s in range(CHUNKS[c] // SUB):
                columns = slice(s * SUB, (s + 1) * SUB)
                f_bank = f_banks.tile([P, PACK, SUB], F32, tag="f_bank")
                for t in range(PACK):
                    nc.tensor.matmul_mx(
                        out=f_bank[:, t, :],
                        lhsT=phi_codes[:, t * P : (t + 1) * P].bitcast(FP8X4),
                        lhsT_scale=phi_scales[:, t * P : (t + 1) * P],
                        rhs=theta[c][1][:, columns].bitcast(FP8X4),
                        rhs_scale=theta[c][2][:, columns],
                        start=True,
                        stop=True,
                    )
                f_filled[c, s] = f_bank

        def empty_f(c, s):
            if s >= CHUNKS[c] // SUB:
                return
            to = f[c][0][:, s * SUB : (s + 1) * SUB, :]
            source = f_filled[c, s][:].rearrange("q t n -> q n t")
            if f_engine(c, s) == "V":
                nc.vector.tensor_scalar_mul(to, source, 1.0 / POOLED)
            else:
                nc.scalar.activation(out=to, in_=source, func=COPY, scale=1.0 / POOLED)

        def quantise_f(c):
            quantise(f[c], 0, CHUNKS[c])

        def transpose_g():
            g_words = g_raw[:].bitcast(F32).rearrange("p b (q u) -> p b u q", u=2)
            for half in range(2):
                g_bank = y_banks.tile([P, 2, 2 * P], F32, tag="y_bank")
                for b in range(2):
                    for u in range(2):
                        nc.tensor.transpose(
                            g_bank[:, u, b * P : (b + 1) * P], g_words[:, 2 * half + b, u, :], identity[:]
                        )
                g_filled[half] = g_bank

        def empty_g(engine, half):
            columns = slice(half * 2 * P, (half + 1) * 2 * P)
            copy(
                engine,
                g_grouped[:].bitcast(F32)[:, columns, :],
                g_filled[half][:].rearrange("q u d -> q d u"),
            )

        def quantise_g():
            quantise((g_grouped, g_codes, g_scales), 0, FEATURES)

        def second_product(c):
            for h in range(N_BLOCKS // PAIR):
                y_bank = y_banks.tile([P, PAIR, CHUNKS[c]], F32, tag="y_bank")
                for b in range(PAIR):
                    rows = slice((h * PAIR + b) * P, (h * PAIR + b + 1) * P)
                    nc.tensor.matmul_mx(
                        out=y_bank[:, b, :],
                        lhsT=g_codes[:, rows].bitcast(FP8X4),
                        lhsT_scale=g_scales[:, rows],
                        rhs=f[c][1][:].bitcast(FP8X4),
                        rhs_scale=f[c][2][:],
                        start=True,
                        stop=True,
                    )
                y_filled[c, h] = y_bank

        def empty_y(c, h):
            y_sb = keep.tile([P, PAIR, CHUNKS[c]], F32, name="y_sb%d_%d" % (c, h))
            copy(y_engine(c, h), y_sb[:], y_filled[c, h][:])
            nc.sync.dma_start(
                out=out_rows[h, :, :, STARTS[c] : STARTS[c] + CHUNKS[c]], in_=y_sb[:]
            )

        def live(c):
            return 0 <= c < N_CHUNKS

        def warm_up():
            warm_bank = f_banks.tile([P, BANK], F32, tag="f_bank")
            moving = [zeros[:]] * WARM_ZEROS + [phi_raw[:, j, :] for j in range(WARM_PHI)]
            for rhs in moving:
                nc.tensor.matmul(warm_bank[:], lhsT=zeros[:, :P], rhs=rhs, start=True, stop=True)

        def f_engine(c, s):
            if c < 2 or c == N_CHUNKS - 1:
                return "S"
            return "VS"[s]

        def y_engine(c, h):
            return "V" if (c, h) in ((N_CHUNKS - 3, 1), (N_CHUNKS - 1, 1)) else "S"

        with tc.manual_schedule():
            warm_up()
            regroup_phi("V", 0, 2)
            regroup_phi("S", 2, 3)
            regroup_phi("V", 3, 4)
            transpose_g()
            regroup_theta(0)
            quantise_phi(0)
            quantise_phi(1)
            quantise_theta(0)
            first_product(0)
            regroup_theta(1)
            empty_g("S", 0)
            empty_g("V", 1)
            for c in range(N_CHUNKS + 1):
                if live(c + 1):
                    quantise_theta(c + 1)
                if live(c):
                    empty_f(c, 0)
                    empty_f(c, 1)
                if live(c - 1):
                    empty_y(c - 1, 0)
                if live(c + 1):
                    first_product(c + 1)
                if live(c + 2):
                    regroup_theta(c + 2)
                if c == 0:
                    quantise_g()
                if live(c):
                    quantise_f(c)
                if live(c - 1):
                    empty_y(c - 1, 1)
                if live(c):
                    second_product(c)
